import numpy as np
import ml_dtypes


def mxq(x, axis, fmt="e4m3"):
    dtype, down = {"e4m3": (ml_dtypes.float8_e4m3fn, 7), "e5m2": (ml_dtypes.float8_e5m2, 14)}[fmt]
    v = np.moveaxis(np.asarray(x, np.float32).astype(ml_dtypes.bfloat16).astype(np.float64), axis, -1)
    blocks = v.reshape(v.shape[:-1] + (-1, 32))
    amax = np.abs(blocks).max(-1, keepdims=True)
    byte = np.maximum(np.where(amax > 0, np.frexp(amax)[1] - 1 + 127, 0) - down, 1)
    scale = np.exp2(byte - 127.0)
    codes = (blocks / scale).astype(np.float32).astype(dtype).astype(np.float64)
    return np.moveaxis((codes * scale).reshape(v.shape), -1, axis)


WIDE = False


def mx_kscale(k):
    if not WIDE:
        return np.ones(k)
    levels = np.array([20, -20, 10, -10, 0])
    a = np.random.permutation(np.resize(levels, k // 512 * 4)).reshape(k // 512, 4)
    idx = np.arange(k)
    return np.exp2(a[idx // 512, idx % 128 // 32])


BF16 = ml_dtypes.bfloat16


def bf(x):
    return np.asarray(x, np.float32).astype(BF16)


def f64(x):
    return np.asarray(x).astype(np.float64)


B, L, F, A = 1024, 3, 1024, 512


def setup_inputs():
    s = mx_kscale(B)[:, None, None]
    x = np.random.standard_normal((B, L, F)) * s
    W = np.random.standard_normal((L, L, F, A)) * 0.016
    g = np.random.standard_normal((B, L, A)) * np.exp2(np.random.randint(-12, 1, (B, L, 1))) / s
    return {"x": bf(x), "W": bf(W), "grad_out": bf(g)}


def reference(x, W, grad_out):
    n = W.shape[0]
    xq = mxq(f64(x), 0, "e4m3")
    gq = mxq(f64(grad_out), 0, "e5m2")
    out = np.zeros(W.shape)
    for i in range(n):
        for j in range(i + 1):
            out[i, j] = xq[:, j, :].T @ gq[:, i, :]
    return out

@@ -1,0 +1,200 @@
+from contextlib import ExitStack
+
+import concourse.mybir as mybir
+
+F32 = mybir.dt.float32
+BF16 = mybir.dt.bfloat16
+U32 = mybir.dt.uint32
+U8 = mybir.dt.uint8
+E4M3X4 = mybir.dt.float8_e4m3fn_x4
+E5M2X4 = mybir.dt.float8_e5m2_x4
+
+B, L, F, A = 1024, 3, 1024, 512
+P = 128
+PACK = 4
+K_PASS = P * PACK
+PASSES = B // K_PASS
+UNIT = 512
+HALVES = F // UNIT
+BLOCKS = [(0, 0), (1, 0), (2, 0), (1, 1), (2, 1), (2, 2)]
+ZERO_BLOCKS = [(0, 1), (0, 2), (1, 2)]
+
+FLOPS = 2 * len(BLOCKS) * B * F * A
+BYTES = 2 * B * L * F + 2 * B * L * A + 4 * L * L * F * A
+
+PINNED = False
+WAYS = 1
+SPLIT_LAST = False
+OUT_BUFS = 8
+STAGE_BUFS = 6
+
+
+def tile_decoder_kernel(tc, x, W, grad_out, out):
+    nc = tc.nc
+    with ExitStack() as ctx:
+        raw = ctx.enter_context(tc.tile_pool(name="raw", bufs=1))
+        keep = ctx.enter_context(tc.tile_pool(name="keep", bufs=1))
+        stage = ctx.enter_context(tc.tile_pool(name="stage", bufs=STAGE_BUFS))
+        outs = ctx.enter_context(tc.tile_pool(name="outs", bufs=OUT_BUFS))
+        psum = ctx.enter_context(tc.psum_pool(name="psum", bufs=8))
+        if PINNED:
+            ctx.enter_context(tc.manual_schedule())
+
+        g_raw = []
+        x_raw = []
+        for c in range(PASSES):
+            g_raw.append(raw.tile([P, PACK, L, A], BF16, name="g_raw%d" % c))
+            x_raw.append(raw.tile([P, PACK, L, F], BF16, name="x_raw%d" % c))
+        for c in range(PASSES):
+            nc.sync.dma_start(
+                out=g_raw[c][:].rearrange("p t l a -> p (t l a)"),
+                in_=grad_out[c * K_PASS : (c + 1) * K_PASS].rearrange("(p t) l a -> p (t l a)", t=PACK),
+            )
+        for c in range(PASSES):
+            rows = x[c * K_PASS : (c + 1) * K_PASS].rearrange("(p t) l f -> p t l f", t=PACK)
+            if SPLIT_LAST and c == PASSES - 1:
+                nc.sync.dma_start(out=x_raw[c][:, :, 0, :], in_=rows[:, :, 0, :])
+                nc.sync.dma_start(
+                    out=x_raw[c][:, :, 1:, :].rearrange("p t l f -> p t (l f)"),
+                    in_=rows[:, :, 1:, :].rearrange("p t l f -> p t (l f)"),
+                )
+            else:
+                nc.sync.dma_start(
+                    out=x_raw[c][:].rearrange("p t l f -> p (t l f)"),
+                    in_=rows.rearrange("p t l f -> p (t l f)"),
+                )
+
+        zeros = keep.tile([P, 8 * A], F32, name="zeros")
+        nc.vector.memset(zeros[:], 0.0)
+        for i, j in ZERO_BLOCKS:
+            nc.sync.dma_start(out=out[i, j].rearrange("(p r) a -> p (r a)", r=8), in_=zeros[:])
+
+        codes = {}
+        planes = {}
+        grouped = {}
+
+        def regroup(key, copy):
+            t = stage.tile([P, UNIT, PACK], BF16, align_bytes=64, name="grouped")
+            grouped[key] = t
+            kind, c, layer, s = key
+            if kind == "g":
+                src = g_raw[c][:, :, layer, :]
+                copy(
+                    out=t[:].rearrange("p (q r) t -> p q t r", r=4),
+                    in_=src.rearrange("p t (q r) -> p q t r", r=4),
+                )
+            elif WAYS == 1:
+                src = x_raw[c][:, :, layer, s * UNIT : (s + 1) * UNIT]
+                copy(
+                    out=t[:].rearrange("p (q r) t -> p q t r", r=4),
+                    in_=src.rearrange("p t (q r) -> p q t r", r=4),
+                )
+            elif WAYS == 4:
+                src = x_raw[c][:, :, layer, s * UNIT : (s + 1) * UNIT]
+                copy(
+                    out=t[:].rearrange("p (m q) t -> p m q t", m=4),
+                    in_=src.rearrange("p t (q m) -> p m q t", m=4),
+                )
+            else:
+                src = x_raw[c][:, :, layer, :].rearrange("p t (q h m) -> p h m q t", h=2, m=4)
+                copy(out=t[:].rearrange("p (m q) t -> p m q t", m=4), in_=src[:, s])
+
+        def quantise(key):
+            kind, c, layer, s = key
+            tag = "%s%d%d%d" % key
+            codes[key] = keep.tile([P, UNIT], U32, align_bytes=64, name="codes_" + tag)
+            planes[key] = keep.tile([P, UNIT], U8, align_bytes=64, name="plane_" + tag)
+            nc.vector.quantize_mx(
+                out=codes[key][:].bitcast(E5M2X4 if kind == "g" else E4M3X4),
+                scales=planes[key][:],
+                in_=grouped[key][:].rearrange("p w t -> p (w t)"),
+            )
+
+        vcopy = nc.vector.tensor_copy
+        scopy = nc.scalar.copy
+
+        for c in range(PASSES):
+            regroup(("g", c, 0, 0), vcopy)
+            regroup(("g", c, 1, 0), vcopy)
+            regroup(("g", c, 2, 0), scopy)
+            for i in range(L):
+                quantise(("g", c, i, 0))
+        regroup(("x", 0, 0, 0), vcopy)
+        regroup(("x", 0, 0, 1), vcopy)
+        regroup(("x", 0, 1, 0), scopy)
+        regroup(("x", 0, 1, 1), scopy)
+        quantise(("x", 0, 0, 0))
+        quantise(("x", 0, 0, 1))
+
+        acc = {}
+
+        def mx_pass(n, c, i, j, s, m):
+            if c == 0:
+                acc[n] = psum.tile([P, A], F32, name="acc")
+            cols = slice(m * P, (m + 1) * P)
+            nc.tensor.matmul_mx(
+                out=acc[n][:],
+                lhsT=codes[("x", c, j, s)][:, cols].bitcast(E4M3X4),
+                lhsT_scale=planes[("x", c, j, s)][:, cols],
+                rhs=codes[("g", c, i, 0)][:].bitcast(E5M2X4),
+                rhs_scale=planes[("g", c, i, 0)][:],
+                start=(c == 0),
+                stop=(c == PASSES - 1),
+            )
+
+        for n in range(8):
+            mx_pass(n, 0, 0, 0, n // 4, n % 4)
+
+        regroup(("x", 1, 0, 0), vcopy)
+        quantise(("x", 1, 0, 0))
+        regroup(("x", 1, 0, 1), vcopy)
+        quantise(("x", 1, 0, 1))
+
+        later = []
+        later.append(("q", ("x", 0, 1, 0)))
+        later.append(("q", ("x", 0, 1, 1)))
+        for c, layer in [(1, 1), (0, 2), (1, 2)]:
+            later.append(("r", ("x", c, layer, 0)))
+            later.append(("r", ("x", c, layer, 1)))
+            later.append(("q", ("x", c, layer, 0)))
+            later.append(("q", ("x", c, layer, 1)))
+        taken = [0]
+
+        def fill(count):
+            for k in range(count):
+                if taken[0] < len(later):
+                    what, key = later[taken[0]]
+                    taken[0] += 1
+                    if what == "r":
+                        regroup(key, vcopy)
+                    else:
+                        quantise(key)
+
+        group_tiles = 8 if WAYS == 8 else 4
+        n = 0
+        o = None
+        for i, j in BLOCKS:
+            while any(("x", c, j, s) not in codes for c in range(PASSES) for s in range(HALVES)):
+                fill(1)
+            for s in range(HALVES):
+                for m in range(4):
+                    if n % group_tiles == 0:
+                        o = outs.tile([P, group_tiles, A], F32, name="o")
+                    if n >= 8:
+                        mx_pass(n, 0, i, j, s, m)
+                    mx_pass(n, 1, i, j, s, m)
+                    on_vector = (n % 8 == 7) if n < 40 else (n % 2 == 1)
+                    (vcopy if on_vector else scopy)(out=o[:, n % group_tiles, :], in_=acc[n][:])
+                    if on_vector:
+                        fill(4)
+                    n += 1
+                    if n % group_tiles == 0:
+                        if WAYS == 1:
+                            dst = out[i, j, s * UNIT : (s + 1) * UNIT, :].rearrange("(m p) a -> p m a", p=P)
+                            nc.sync.dma_start(out=dst, in_=o[:])
+                        elif WAYS == 4:
+                            dst = out[i, j, s * UNIT : (s + 1) * UNIT, :].rearrange("(p m) a -> p (m a)", m=4)
+                            nc.sync.dma_start(out=dst, in_=o[:].rearrange("p m a -> p (m a)"))
+                        else:
+                            dst = out[i, j].rearrange("(p m) a -> p (m a)", m=8)
+                            nc.sync.dma_start(out=dst, in_=o[:].rearrange("p m a -> p (m a)"))

@@ -23,7 +23,7 @@ FLOPS = 2 * len(BLOCKS) * B * F * A
 BYTES = 2 * B * L * F + 2 * B * L * A + 4 * L * L * F * A
 
 PINNED = False
-WAYS = 1
+WAYS = 4
 SPLIT_LAST = False
 OUT_BUFS = 8
 STAGE_BUFS = 6

@@ -22,7 +22,7 @@ ZERO_BLOCKS = [(0, 1), (0, 2), (1, 2)]
 FLOPS = 2 * len(BLOCKS) * B * F * A
 BYTES = 2 * B * L * F + 2 * B * L * A + 4 * L * L * F * A
 
-PINNED = False
+PINNED = True
 WAYS = 4
 SPLIT_LAST = False
 OUT_BUFS = 8

@@ -24,7 +24,7 @@ BYTES = 2 * B * L * F + 2 * B * L * A + 4 * L * L * F * A
 
 PINNED = True
 WAYS = 4
-SPLIT_LAST = False
+SPLIT_LAST = True
 OUT_BUFS = 8
 STAGE_BUFS = 6
 

@@ -23,9 +23,9 @@ FLOPS = 2 * len(BLOCKS) * B * F * A
 BYTES = 2 * B * L * F + 2 * B * L * A + 4 * L * L * F * A
 
 PINNED = True
-WAYS = 4
-SPLIT_LAST = True
-OUT_BUFS = 8
+WAYS = 8
+SPLIT_LAST = False
+OUT_BUFS = 4
 STAGE_BUFS = 6
 
 
@@ -195,6 +195,11 @@ def tile_decoder_kernel(tc, x, W, grad_out, out):
                         elif WAYS == 4:
                             dst = out[i, j, s * UNIT : (s + 1) * UNIT, :].rearrange("(p m) a -> p (m a)", m=4)
                             nc.sync.dma_start(out=dst, in_=o[:].rearrange("p m a -> p (m a)"))
-                        else:
+                        elif (i, j) != BLOCKS[-1]:
                             dst = out[i, j].rearrange("(p m) a -> p (m a)", m=8)
                             nc.sync.dma_start(out=dst, in_=o[:].rearrange("p m a -> p (m a)"))
+                    if WAYS == 8 and (i, j) == BLOCKS[-1] and n % 4 == 0:
+                        dst = out[i, j].rearrange("(p h m) a -> p h (m a)", h=2, m=4)
+                        nc.sync.dma_start(
+                            out=dst[:, s], in_=o[:, 4 * s : 4 * s + 4, :].rearrange("p m a -> p (m a)")
+                        )

@@ -23,9 +23,9 @@ FLOPS = 2 * len(BLOCKS) * B * F * A
 BYTES = 2 * B * L * F + 2 * B * L * A + 4 * L * L * F * A
 
 PINNED = True
-WAYS = 8
+WAYS = 4
 SPLIT_LAST = False
-OUT_BUFS = 4
+OUT_BUFS = 8
 STAGE_BUFS = 6
 
 
@@ -92,8 +92,8 @@ def tile_decoder_kernel(tc, x, W, grad_out, out):
             elif WAYS == 4:
                 src = x_raw[c][:, :, layer, s * UNIT : (s + 1) * UNIT]
                 copy(
-                    out=t[:].rearrange("p (m q) t -> p m q t", m=4),
-                    in_=src.rearrange("p t (q m) -> p m q t", m=4),
+                    out=t[:].rearrange("p (m q) t -> p q t m", m=4),
+                    in_=src.rearrange("p t (q m) -> p q t m", m=4),
                 )
             else:
                 src = x_raw[c][:, :, layer, :].rearrange("p t (q h m) -> p h m q t", h=2, m=4)
@@ -195,11 +195,6 @@ def tile_decoder_kernel(tc, x, W, grad_out, out):
                         elif WAYS == 4:
                             dst = out[i, j, s * UNIT : (s + 1) * UNIT, :].rearrange("(p m) a -> p (m a)", m=4)
                             nc.sync.dma_start(out=dst, in_=o[:].rearrange("p m a -> p (m a)"))
-                        elif (i, j) != BLOCKS[-1]:
+                        else:
                             dst = out[i, j].rearrange("(p m) a -> p (m a)", m=8)
                             nc.sync.dma_start(out=dst, in_=o[:].rearrange("p m a -> p (m a)"))
-                    if WAYS == 8 and (i, j) == BLOCKS[-1] and n % 4 == 0:
-                        dst = out[i, j].rearrange("(p h m) a -> p h (m a)", h=2, m=4)
-                        nc.sync.dma_start(
-                            out=dst[:, s], in_=o[:, 4 * s : 4 * s + 4, :].rearrange("p m a -> p (m a)")
-                        )

@@ -23,9 +23,9 @@ FLOPS = 2 * len(BLOCKS) * B * F * A
 BYTES = 2 * B * L * F + 2 * B * L * A + 4 * L * L * F * A
 
 PINNED = True
-WAYS = 4
+WAYS = 8
 SPLIT_LAST = False
-OUT_BUFS = 8
+OUT_BUFS = 4
 STAGE_BUFS = 6
 
 
@@ -92,12 +92,12 @@ def tile_decoder_kernel(tc, x, W, grad_out, out):
             elif WAYS == 4:
                 src = x_raw[c][:, :, layer, s * UNIT : (s + 1) * UNIT]
                 copy(
-                    out=t[:].rearrange("p (m q) t -> p q t m", m=4),
-                    in_=src.rearrange("p t (q m) -> p q t m", m=4),
+                    out=t[:].rearrange("p (m q) t -> p m q t", m=4),
+                    in_=src.rearrange("p t (q m) -> p m q t", m=4),
                 )
             else:
-                src = x_raw[c][:, :, layer, :].rearrange("p t (q h m) -> p h m q t", h=2, m=4)
-                copy(out=t[:].rearrange("p (m q) t -> p m q t", m=4), in_=src[:, s])
+                src = x_raw[c][:, :, layer, :].rearrange("p t (q h m) -> p h q t m", h=2, m=4)
+                copy(out=t[:].rearrange("p (m q) t -> p q t m", m=4), in_=src[:, s])
 
         def quantise(key):
             kind, c, layer, s = key
@@ -195,6 +195,11 @@ def tile_decoder_kernel(tc, x, W, grad_out, out):
                         elif WAYS == 4:
                             dst = out[i, j, s * UNIT : (s + 1) * UNIT, :].rearrange("(p m) a -> p (m a)", m=4)
                             nc.sync.dma_start(out=dst, in_=o[:].rearrange("p m a -> p (m a)"))
-                        else:
+                        elif (i, j) != BLOCKS[-1]:
                             dst = out[i, j].rearrange("(p m) a -> p (m a)", m=8)
                             nc.sync.dma_start(out=dst, in_=o[:].rearrange("p m a -> p (m a)"))
+                    if WAYS == 8 and (i, j) == BLOCKS[-1] and n % 4 == 0:
+                        dst = out[i, j].rearrange("(p h m) a -> p h (m a)", h=2, m=4)
+                        nc.sync.dma_start(
+                            out=dst[:, s], in_=o[:, 4 * s : 4 * s + 4, :].rearrange("p m a -> p (m a)")
+                        )

from contextlib import ExitStack

import concourse.mybir as mybir

F32 = mybir.dt.float32
BF16 = mybir.dt.bfloat16
U32 = mybir.dt.uint32
U8 = mybir.dt.uint8
E4M3X4 = mybir.dt.float8_e4m3fn_x4
E5M2X4 = mybir.dt.float8_e5m2_x4

B, L, F, A = 1024, 3, 1024, 512
P = 128
PACK = 4
K_PASS = P * PACK
PASSES = B // K_PASS
UNIT = 512
HALVES = F // UNIT
BLOCKS = [(0, 0), (1, 0), (2, 0), (1, 1), (2, 1), (2, 2)]
ZERO_BLOCKS = [(0, 1), (0, 2), (1, 2)]

FLOPS = 2 * len(BLOCKS) * B * F * A
BYTES = 2 * B * L * F + 2 * B * L * A + 4 * L * L * F * A

PINNED = True
WAYS = 8
SPLIT_LAST = False
OUT_BUFS = 4
STAGE_BUFS = 6


def tile_decoder_kernel(tc, x, W, grad_out, out):
    nc = tc.nc
    with ExitStack() as ctx:
        raw = ctx.enter_context(tc.tile_pool(name="raw", bufs=1))
        keep = ctx.enter_context(tc.tile_pool(name="keep", bufs=1))
        stage = ctx.enter_context(tc.tile_pool(name="stage", bufs=STAGE_BUFS))
        outs = ctx.enter_context(tc.tile_pool(name="outs", bufs=OUT_BUFS))
        psum = ctx.enter_context(tc.psum_pool(name="psum", bufs=8))
        if PINNED:
            ctx.enter_context(tc.manual_schedule())

        g_raw = []
        x_raw = []
        for c in range(PASSES):
            g_raw.append(raw.tile([P, PACK, L, A], BF16, name="g_raw%d" % c))
            x_raw.append(raw.tile([P, PACK, L, F], BF16, name="x_raw%d" % c))
        for c in range(PASSES):
            nc.sync.dma_start(
                out=g_raw[c][:].rearrange("p t l a -> p (t l a)"),
                in_=grad_out[c * K_PASS : (c + 1) * K_PASS].rearrange("(p t) l a -> p (t l a)", t=PACK),
            )
        for c in range(PASSES):
            rows = x[c * K_PASS : (c + 1) * K_PASS].rearrange("(p t) l f -> p t l f", t=PACK)
            if SPLIT_LAST and c == PASSES - 1:
                nc.sync.dma_start(out=x_raw[c][:, :, 0, :], in_=rows[:, :, 0, :])
                nc.sync.dma_start(
                    out=x_raw[c][:, :, 1:, :].rearrange("p t l f -> p t (l f)"),
                    in_=rows[:, :, 1:, :].rearrange("p t l f -> p t (l f)"),
                )
            else:
                nc.sync.dma_start(
                    out=x_raw[c][:].rearrange("p t l f -> p (t l f)"),
                    in_=rows.rearrange("p t l f -> p (t l f)"),
                )

        zeros = keep.tile([P, 8 * A], F32, name="zeros")
        nc.vector.memset(zeros[:], 0.0)
        for i, j in ZERO_BLOCKS:
            nc.sync.dma_start(out=out[i, j].rearrange("(p r) a -> p (r a)", r=8), in_=zeros[:])

        codes = {}
        planes = {}
        grouped = {}

        def regroup(key, copy):
            t = stage.tile([P, UNIT, PACK], BF16, align_bytes=64, name="grouped")
            grouped[key] = t
            kind, c, layer, s = key
            if kind == "g":
                src = g_raw[c][:, :, layer, :]
                copy(
                    out=t[:].rearrange("p (q r) t -> p q t r", r=4),
                    in_=src.rearrange("p t (q r) -> p q t r", r=4),
                )
            elif WAYS == 1:
                src = x_raw[c][:, :, layer, s * UNIT : (s + 1) * UNIT]
                copy(
                    out=t[:].rearrange("p (q r) t -> p q t r", r=4),
                    in_=src.rearrange("p t (q r) -> p q t r", r=4),
                )
            elif WAYS == 4:
                src = x_raw[c][:, :, layer, s * UNIT : (s + 1) * UNIT]
                copy(
                    out=t[:].rearrange("p (m q) t -> p m q t", m=4),
                    in_=src.rearrange("p t (q m) -> p m q t", m=4),
                )
            else:
                src = x_raw[c][:, :, layer, :].rearrange("p t (q h m) -> p h q t m", h=2, m=4)
                copy(out=t[:].rearrange("p (m q) t -> p q t m", m=4), in_=src[:, s])

        def quantise(key):
            kind, c, layer, s = key
            tag = "%s%d%d%d" % key
            codes[key] = keep.tile([P, UNIT], U32, align_bytes=64, name="codes_" + tag)
            planes[key] = keep.tile([P, UNIT], U8, align_bytes=64, name="plane_" + tag)
            nc.vector.quantize_mx(
                out=codes[key][:].bitcast(E5M2X4 if kind == "g" else E4M3X4),
                scales=planes[key][:],
                in_=grouped[key][:].rearrange("p w t -> p (w t)"),
            )

        vcopy = nc.vector.tensor_copy
        scopy = nc.scalar.copy

        for c in range(PASSES):
            regroup(("g", c, 0, 0), vcopy)
            regroup(("g", c, 1, 0), vcopy)
            regroup(("g", c, 2, 0), scopy)
            for i in range(L):
                quantise(("g", c, i, 0))
        regroup(("x", 0, 0, 0), vcopy)
        regroup(("x", 0, 0, 1), vcopy)
        regroup(("x", 0, 1, 0), scopy)
        regroup(("x", 0, 1, 1), scopy)
        quantise(("x", 0, 0, 0))
        quantise(("x", 0, 0, 1))

        acc = {}

        def mx_pass(n, c, i, j, s, m):
            if c == 0:
                acc[n] = psum.tile([P, A], F32, name="acc")
            cols = slice(m * P, (m + 1) * P)
            nc.tensor.matmul_mx(
                out=acc[n][:],
                lhsT=codes[("x", c, j, s)][:, cols].bitcast(E4M3X4),
                lhsT_scale=planes[("x", c, j, s)][:, cols],
                rhs=codes[("g", c, i, 0)][:].bitcast(E5M2X4),
                rhs_scale=planes[("g", c, i, 0)][:],
                start=(c == 0),
                stop=(c == PASSES - 1),
            )

        for n in range(8):
            mx_pass(n, 0, 0, 0, n // 4, n % 4)

        regroup(("x", 1, 0, 0), vcopy)
        quantise(("x", 1, 0, 0))
        regroup(("x", 1, 0, 1), vcopy)
        quantise(("x", 1, 0, 1))

        later = []
        later.append(("q", ("x", 0, 1, 0)))
        later.append(("q", ("x", 0, 1, 1)))
        for c, layer in [(1, 1), (0, 2), (1, 2)]:
            later.append(("r", ("x", c, layer, 0)))
            later.append(("r", ("x", c, layer, 1)))
            later.append(("q", ("x", c, layer, 0)))
            later.append(("q", ("x", c, layer, 1)))
        taken = [0]

        def fill(count):
            for k in range(count):
                if taken[0] < len(later):
                    what, key = later[taken[0]]
                    taken[0] += 1
                    if what == "r":
                        regroup(key, vcopy)
                    else:
                        quantise(key)

        group_tiles = 8 if WAYS == 8 else 4
        n = 0
        o = None
        for i, j in BLOCKS:
            while any(("x", c, j, s) not in codes for c in range(PASSES) for s in range(HALVES)):
                fill(1)
            for s in range(HALVES):
                for m in range(4):
                    if n % group_tiles == 0:
                        o = outs.tile([P, group_tiles, A], F32, name="o")
                    if n >= 8:
                        mx_pass(n, 0, i, j, s, m)
                    mx_pass(n, 1, i, j, s, m)
                    on_vector = (n % 8 == 7) if n < 40 else (n % 2 == 1)
                    (vcopy if on_vector else scopy)(out=o[:, n % group_tiles, :], in_=acc[n][:])
                    if on_vector:
                        fill(4)
                    n += 1
                    if n % group_tiles == 0:
                        if WAYS == 1:
                            dst = out[i, j, s * UNIT : (s + 1) * UNIT, :].rearrange("(m p) a -> p m a", p=P)
                            nc.sync.dma_start(out=dst, in_=o[:])
                        elif WAYS == 4:
                            dst = out[i, j, s * UNIT : (s + 1) * UNIT, :].rearrange("(p m) a -> p (m a)", m=4)
                            nc.sync.dma_start(out=dst, in_=o[:].rearrange("p m a -> p (m a)"))
                        elif (i, j) != BLOCKS[-1]:
                            dst = out[i, j].rearrange("(p m) a -> p (m a)", m=8)
                            nc.sync.dma_start(out=dst, in_=o[:].rearrange("p m a -> p (m a)"))
                    if WAYS == 8 and (i, j) == BLOCKS[-1] and n % 4 == 0:
                        dst = out[i, j].rearrange("(p h m) a -> p h (m a)", h=2, m=4)
                        nc.sync.dma_start(
                            out=dst[:, s], in_=o[:, 4 * s : 4 * s + 4, :].rearrange("p m a -> p (m a)")
                        )
